import numpy as np
import ml_dtypes

BF16 = ml_dtypes.bfloat16


def bf(x):
    return np.asarray(x, np.float32).astype(BF16)


def f32(x):
    return np.asarray(x, np.float32)


def f64(x):
    return np.asarray(x).astype(np.float64)


def striped(idx):
    return np.tile(idx.reshape(-1, 16).T, (8, 1))


S, D, H, M, K, T, LV, N = 4096, 128, 128, 512, 4096, 128, 4, 1920


def sigmoid(v):
    return 1.0 / (1.0 + np.exp(-v))


def setup_inputs():
    return {
        "table": bf(np.random.standard_normal((S, D))),
        "w": bf(np.random.standard_normal((D, M)) / np.sqrt(D)),
        "b": f32(0.2 * np.random.standard_normal((M, 1))),
        "u_iou": bf(2.0 * np.random.standard_normal((H, M - H)) / np.sqrt(H)),
        "u_f": bf(2.0 * np.random.standard_normal((H, H)) / np.sqrt(H)),
        "w_out": bf(4.0 * np.random.standard_normal((H, K)) / np.sqrt(H)),
        "b_out": f32(0.1 * np.random.standard_normal((K, 1))),
        "offs": striped(np.random.permutation(np.tile(np.arange(S), 2))[:N]),
    }


def reference(table, w, b, u_iou, u_f, w_out, b_out, offs):
    idx = offs[:16].T.reshape(-1)
    pre = f64(w).T @ f64(table)[idx].T + f64(b)
    h = np.zeros((H, N))
    c = np.zeros((H, N))
    for lv in range(LV - 1, -1, -1):
        lo, hi = T * (2**lv - 1), T * (2 ** (lv + 1) - 1)
        iou = pre[: M - H, lo:hi]
        fc = 0.0
        if lv < LV - 1:
            hc = h[:, 2 * lo + T : 2 * hi + T]
            cc = c[:, 2 * lo + T : 2 * hi + T]
            iou = iou + f64(u_iou).T @ (hc[:, 0::2] + hc[:, 1::2])
            f = sigmoid(np.repeat(pre[M - H :, lo:hi], 2, axis=1) + f64(u_f).T @ hc)
            fc = (f * cc)[:, 0::2] + (f * cc)[:, 1::2]
        c[:, lo:hi] = sigmoid(iou[:H]) * np.tanh(iou[2 * H :]) + fc
        h[:, lo:hi] = sigmoid(iou[H : 2 * H]) * np.tanh(c[:, lo:hi])
    return f64(w_out).T @ h + f64(b_out)

@@ -1,0 +1,198 @@
+import concourse.mybir as mybir
+from concourse.masks import make_identity
+
+BF16, F32, U16 = mybir.dt.bfloat16, mybir.dt.float32, mybir.dt.uint16
+SIGMOID = mybir.ActivationFunctionType.Sigmoid
+TANH = mybir.ActivationFunctionType.Tanh
+IDENTITY = mybir.ActivationFunctionType.Identity
+
+P = 128
+WORDS, CLASSES, N = 4096, 4096, 1920
+GATE_I, GATE_O, GATE_U, GATE_F = 0, 1, 2, 3
+LEVEL1, LEVEL2, LEAVES = 128, 384, 896
+PIECE = 512
+BLOCKS = CLASSES // P
+ROWS = 8
+CHUNK = P * ROWS
+EARLY_BLOCKS = 16
+
+FLOPS = 2 * P * (4 * P * N + 3 * P * LEAVES + P * 2 * LEAVES + CLASSES * N)
+
+
+def tile_treemodel_b_kernel(tc, table, w, b, u_iou, u_f, w_out, b_out, offs, out):
+    nc = tc.nc
+    with (
+        tc.tile_pool(name="held", bufs=1) as held,
+        tc.tile_pool(name="rows", bufs=4) as rows_pool,
+        tc.tile_pool(name="work", bufs=2) as work,
+        tc.tile_pool(name="stage", bufs=12) as stage_pool,
+        tc.psum_pool(name="psum", bufs=8) as psum,
+    ):
+        offsets = held.tile([P, N // 16], U16, name="offsets")
+        nc.sync.dma_start(offsets[:], offs)
+        w_sb = held.tile([P, 4 * P], BF16, name="w_sb")
+        nc.scalar.dma_start(w_sb[:], w)
+
+        identity = held.tile([P, P], BF16, name="identity")
+        make_identity(nc, identity[:])
+
+        chunks = []
+        for g in range(WORDS // CHUNK):
+            rows = rows_pool.tile([P, ROWS * P], BF16, name="rows")
+            queue = nc.sync if g % 2 == 0 else nc.scalar
+            queue.dma_start(
+                rows[:], table[g * CHUNK : (g + 1) * CHUNK, :].rearrange("(p r) d -> p (r d)", r=ROWS)
+            )
+            chunks.append(rows)
+
+        b_sb = held.tile([P, 4], F32, name="b_sb")
+        with nc.allow_non_contiguous_dma(reason="512 biases, one to a partition and gate"):
+            nc.gpsimd.dma_start(b_sb[:], b.rearrange("(g p) o -> p (g o)", p=P))
+        b_out_rows = held.tile([P, BLOCKS], F32, name="b_out_rows", align_bytes=64)
+        b_out_sb = held.tile([P, BLOCKS], F32, name="b_out_sb", align_bytes=64)
+        b_out_view = b_out.rearrange("(a q i) o -> q a (i o)", q=4, i=32)
+        for q in range(4):
+            nc.gpsimd.dma_start(b_out_rows[32 * q : 32 * (q + 1), :], b_out_view[q])
+        nc.vector.transpose(b_out_sb[:], b_out_rows[:])
+
+        u_iou_sb = held.tile([P, 3 * P], BF16, name="u_iou_sb")
+        nc.scalar.dma_start(u_iou_sb[:], u_iou)
+        u_f_sb = held.tile([P, P], BF16, name="u_f_sb")
+        nc.scalar.dma_start(u_f_sb[:], u_f)
+        w_out_sb = held.tile([P, CLASSES], BF16, name="w_out_sb")
+        half = CLASSES // 2
+        nc.sync.dma_start(w_out_sb[:, :half], w_out[:, :half])
+        nc.scalar.dma_start(w_out_sb[:, half:], w_out[:, half:])
+
+        table_t = held.tile([P, WORDS], BF16, name="table_t")
+        for g, rows in enumerate(chunks):
+            flipped = psum.tile([P, CHUNK], BF16, name="flipped", tag="bank")
+            for r in range(ROWS):
+                nc.tensor.transpose(flipped[:, r * P : (r + 1) * P], rows[:, r * P : (r + 1) * P], identity[:])
+            nc.vector.tensor_copy(
+                table_t[:, g * CHUNK : (g + 1) * CHUNK].rearrange("d (p r) -> d p r", r=ROWS),
+                flipped[:].rearrange("d (r p) -> d p r", r=ROWS),
+            )
+
+        h = held.tile([P, N], BF16, name="h")
+        c = held.tile([P, N], F32, name="c")
+        pre_sb = held.tile([P, 4, LEAVES], F32, name="pre_sb")
+
+        def project(gate, first, count):
+            bank = psum.tile([P, count], F32, name="bank", tag="bank")
+            nc.tensor.matmul(
+                bank[:],
+                w_sb[:, gate * P : (gate + 1) * P],
+                table_t[:].indirect(offsets[:, first // 16 : (first + count) // 16]),
+                start=True,
+                stop=True,
+            )
+            return bank
+
+        def finish_cell(nodes, gate_o):
+            tanh_c = work.tile([P, nodes.stop - nodes.start], F32, name="tanh_c")
+            nc.scalar.activation(tanh_c[:], c[:, nodes], TANH)
+            nc.vector.tensor_mul(h[:, nodes], gate_o[:], tanh_c[:])
+
+        def leaves(first):
+            nodes = slice(first, first + PIECE)
+            pre_i = project(GATE_I, first, PIECE)
+            pre_u = project(GATE_U, first, PIECE)
+            pre_o = project(GATE_O, first, PIECE)
+            gate_i = work.tile([P, PIECE], F32, name="gate_i")
+            gate_u = work.tile([P, PIECE], F32, name="gate_u")
+            gate_o = work.tile([P, PIECE], F32, name="gate_o")
+            nc.scalar.activation(gate_i[:], pre_i[:], SIGMOID, bias=b_sb[:, GATE_I : GATE_I + 1])
+            nc.scalar.activation(gate_u[:], pre_u[:], TANH, bias=b_sb[:, GATE_U : GATE_U + 1])
+            nc.vector.tensor_mul(c[:, nodes], gate_i[:], gate_u[:])
+            nc.scalar.activation(gate_o[:], pre_o[:], SIGMOID, bias=b_sb[:, GATE_O : GATE_O + 1])
+            finish_cell(nodes, gate_o)
+
+        def project_upper(first, count):
+            for gate in range(4):
+                bank = project(gate, first, count)
+                kept = pre_sb[:, gate, first : first + count]
+                bias = b_sb[:, gate : gate + 1]
+                if gate % 2 == 0:
+                    nc.scalar.activation(kept, bank[:], IDENTITY, bias=bias)
+                else:
+                    nc.vector.tensor_scalar_add(kept, bank[:], bias)
+
+        def level(first, count):
+            nodes = slice(first, first + count)
+            kid0 = 2 * first + P
+            kids = slice(kid0, kid0 + 2 * count)
+            pairs = h[:, kids].rearrange("q (n two) -> q n two", two=2)
+            gates = {}
+            for gate, func in ((GATE_I, SIGMOID), (GATE_U, TANH), (GATE_O, SIGMOID)):
+                bank = psum.tile([P, count], F32, name="bank", tag="bank")
+                for child in range(2):
+                    nc.tensor.matmul(
+                        bank[:],
+                        u_iou_sb[:, gate * P : (gate + 1) * P],
+                        pairs[:, :, child],
+                        start=(child == 0),
+                        stop=(child == 1),
+                    )
+                gates[gate] = work.tile([P, count], F32, name="gate_%d" % gate)
+                nc.vector.tensor_add(gates[gate][:], bank[:], pre_sb[:, gate, nodes])
+                nc.scalar.activation(gates[gate][:], gates[gate][:], func)
+            forget = work.tile([P, 2 * count], F32, name="forget")
+            width = min(PIECE, 2 * count)
+            for k in range(0, 2 * count, width):
+                bank = psum.tile([P, width], F32, name="bank", tag="bank")
+                nc.tensor.matmul(bank[:], u_f_sb[:], h[:, kid0 + k : kid0 + k + width], start=True, stop=True)
+                parents = pre_sb[:, GATE_F, first + k // 2 : first + (k + width) // 2]
+                nc.vector.tensor_add(
+                    forget[:, k : k + width].rearrange("m (n two) -> m n two", two=2),
+                    bank[:].rearrange("m (n two) -> m n two", two=2),
+                    parents.unsqueeze(2).to_broadcast([P, width // 2, 2]),
+                )
+            nc.scalar.activation(forget[:], forget[:], SIGMOID)
+            nc.vector.tensor_mul(forget[:], forget[:], c[:, kids])
+            kept = forget[:].rearrange("m (n two) -> m n two", two=2)
+            nc.vector.tensor_mul(c[:, nodes], gates[GATE_I][:], gates[GATE_U][:])
+            nc.vector.tensor_add(c[:, nodes], c[:, nodes], kept[:, :, 0])
+            nc.vector.tensor_add(c[:, nodes], c[:, nodes], kept[:, :, 1])
+            finish_cell(nodes, gates[GATE_O])
+
+        def classify(block, first, count, staged, turn):
+            bank = psum.tile([P, count], F32, name="bank", tag="bank")
+            nc.tensor.matmul(
+                bank[:], w_out_sb[:, block * P : (block + 1) * P], h[:, first : first + count], start=True, stop=True
+            )
+            bias = b_out_sb[:, block : block + 1]
+            if turn == 0:
+                nc.scalar.activation(staged, bank[:], IDENTITY, bias=bias)
+            else:
+                nc.vector.tensor_scalar_add(staged, bank[:], bias)
+
+        def classify_leaves(block):
+            stage = stage_pool.tile([P, 2, PIECE], F32, name="stage")
+            for turn in range(2):
+                classify(block, LEAVES + turn * PIECE, PIECE, stage[:, turn, :], turn)
+            nc.sync.dma_start(out[block * P : (block + 1) * P, LEAVES:N], stage[:].rearrange("p t n -> p (t n)"))
+
+        def classify_upper(block, first, count):
+            stage = stage_pool.tile([P, 2, count], F32, name="stage")
+            for turn in range(2):
+                classify(block + turn, first, count, stage[:, turn, :], turn)
+            nc.sync.dma_start(
+                out[block * P : (block + 2) * P, first : first + count].rearrange("(t p) n -> p t n", p=P), stage[:]
+            )
+
+        for first in range(LEAVES, N, PIECE):
+            leaves(first)
+        for block in range(EARLY_BLOCKS):
+            classify_leaves(block)
+        project_upper(LEVEL2, LEAVES - LEVEL2)
+        project_upper(0, LEVEL2)
+        level(LEVEL2, LEAVES - LEVEL2)
+        level(LEVEL1, LEVEL2 - LEVEL1)
+        level(0, LEVEL1)
+        for block in range(EARLY_BLOCKS, BLOCKS):
+            classify_leaves(block)
+        for block in range(0, BLOCKS, 2):
+            classify_upper(block, LEVEL2, LEAVES - LEVEL2)
+        for block in range(0, BLOCKS, 2):
+            classify_upper(block, 0, LEVEL2)

@@ -12,8 +12,11 @@ GATE_I, GATE_O, GATE_U, GATE_F = 0, 1, 2, 3
 LEVEL1, LEVEL2, LEAVES = 128, 384, 896
 PIECE = 512
 BLOCKS = CLASSES // P
-ROWS = 8
-CHUNK = P * ROWS
+ROWS = 4
+FLIP = P * ROWS
+UNITS = 2
+SPANS = ((0, LEVEL2), (LEVEL2, PIECE), (LEAVES, PIECE), (LEAVES + PIECE, PIECE))
+FIRST_BLOCKS = 4
 EARLY_BLOCKS = 16
 
 FLOPS = 2 * P * (4 * P * N + 3 * P * LEAVES + P * 2 * LEAVES + CLASSES * N)
@@ -25,57 +28,61 @@ def tile_treemodel_b_kernel(tc, table, w, b, u_iou, u_f, w_out, b_out, offs, out
         tc.tile_pool(name="held", bufs=1) as held,
         tc.tile_pool(name="rows", bufs=4) as rows_pool,
         tc.tile_pool(name="work", bufs=2) as work,
-        tc.tile_pool(name="stage", bufs=12) as stage_pool,
+        tc.tile_pool(name="stage", bufs=17) as stage_pool,
         tc.psum_pool(name="psum", bufs=8) as psum,
     ):
-        offsets = held.tile([P, N // 16], U16, name="offsets")
-        nc.sync.dma_start(offsets[:], offs)
-        w_sb = held.tile([P, 4 * P], BF16, name="w_sb")
-        nc.scalar.dma_start(w_sb[:], w)
+        loaded = []
+        for g in range(WORDS // (UNITS * FLIP)):
+            rows = rows_pool.tile([P, UNITS, ROWS * P], BF16, name="rows")
+            queue = nc.sync if g % 2 == 0 else nc.scalar
+            queue.dma_start(
+                rows[:],
+                table[g * UNITS * FLIP : (g + 1) * UNITS * FLIP, :].rearrange("(u p r) d -> p u (r d)", u=UNITS, r=ROWS),
+            )
+            loaded.append(rows)
 
         identity = held.tile([P, P], BF16, name="identity")
         make_identity(nc, identity[:])
 
-        chunks = []
-        for g in range(WORDS // CHUNK):
-            rows = rows_pool.tile([P, ROWS * P], BF16, name="rows")
-            queue = nc.sync if g % 2 == 0 else nc.scalar
-            queue.dma_start(
-                rows[:], table[g * CHUNK : (g + 1) * CHUNK, :].rearrange("(p r) d -> p (r d)", r=ROWS)
-            )
-            chunks.append(rows)
-
+        offsets = held.tile([P, N // 16], U16, name="offsets")
+        nc.sync.dma_start(offsets[:], offs)
+        w_sb = held.tile([P, 4 * P], BF16, name="w_sb")
+        nc.scalar.dma_start(w_sb[:], w)
         b_sb = held.tile([P, 4], F32, name="b_sb")
         with nc.allow_non_contiguous_dma(reason="512 biases, one to a partition and gate"):
-            nc.gpsimd.dma_start(b_sb[:], b.rearrange("(g p) o -> p (g o)", p=P))
+            nc.scalar.dma_start(b_sb[:], b.rearrange("(g p) o -> p (g o)", p=P))
+        w_out_sb = held.tile([P, CLASSES], BF16, name="w_out_sb")
+        nc.sync.dma_start(w_out_sb[:], w_out)
         b_out_rows = held.tile([P, BLOCKS], F32, name="b_out_rows", align_bytes=64)
         b_out_sb = held.tile([P, BLOCKS], F32, name="b_out_sb", align_bytes=64)
         b_out_view = b_out.rearrange("(a q i) o -> q a (i o)", q=4, i=32)
         for q in range(4):
             nc.gpsimd.dma_start(b_out_rows[32 * q : 32 * (q + 1), :], b_out_view[q])
-        nc.vector.transpose(b_out_sb[:], b_out_rows[:])
-
         u_iou_sb = held.tile([P, 3 * P], BF16, name="u_iou_sb")
-        nc.scalar.dma_start(u_iou_sb[:], u_iou)
+        nc.gpsimd.dma_start(u_iou_sb[:], u_iou)
         u_f_sb = held.tile([P, P], BF16, name="u_f_sb")
-        nc.scalar.dma_start(u_f_sb[:], u_f)
-        w_out_sb = held.tile([P, CLASSES], BF16, name="w_out_sb")
-        half = CLASSES // 2
-        nc.sync.dma_start(w_out_sb[:, :half], w_out[:, :half])
-        nc.scalar.dma_start(w_out_sb[:, half:], w_out[:, half:])
+        nc.gpsimd.dma_start(u_f_sb[:], u_f)
 
         table_t = held.tile([P, WORDS], BF16, name="table_t")
-        for g, rows in enumerate(chunks):
-            flipped = psum.tile([P, CHUNK], BF16, name="flipped", tag="bank")
+        for f in range(WORDS // FLIP):
+            rows = loaded[f // UNITS][:, f % UNITS, :]
+            flipped = psum.tile([P, FLIP], BF16, name="flipped", tag="bank")
             for r in range(ROWS):
                 nc.tensor.transpose(flipped[:, r * P : (r + 1) * P], rows[:, r * P : (r + 1) * P], identity[:])
             nc.vector.tensor_copy(
-                table_t[:, g * CHUNK : (g + 1) * CHUNK].rearrange("d (p r) -> d p r", r=ROWS),
+                table_t[:, f * FLIP : (f + 1) * FLIP].rearrange("d (p r) -> d p r", r=ROWS),
                 flipped[:].rearrange("d (r p) -> d p r", r=ROWS),
             )
 
-        h = held.tile([P, N], BF16, name="h")
-        c = held.tile([P, N], F32, name="c")
+        nc.vector.transpose(b_out_sb[:], b_out_rows[:])
+
+        h_tiles = {first: held.tile([P, count], BF16, name="h_%d" % first) for first, count in SPANS}
+        c_tiles = {first: held.tile([P, count], F32, name="c_%d" % first) for first, count in SPANS}
+
+        def view(tiles, first, count):
+            for start, width in SPANS:
+                if start <= first and first + count <= start + width:
+                    return tiles[start][:, first - start : first - start + count]
         pre_sb = held.tile([P, 4, LEAVES], F32, name="pre_sb")
 
         def project(gate, first, count):
@@ -89,24 +96,20 @@ def tile_treemodel_b_kernel(tc, table, w, b, u_iou, u_f, w_out, b_out, offs, out
             )
             return bank
 
-        def finish_cell(nodes, gate_o):
-            tanh_c = work.tile([P, nodes.stop - nodes.start], F32, name="tanh_c")
-            nc.scalar.activation(tanh_c[:], c[:, nodes], TANH)
-            nc.vector.tensor_mul(h[:, nodes], gate_o[:], tanh_c[:])
+        def finish_cell(first, count, gate_o):
+            tanh_c = work.tile([P, count], F32, name="tanh_c")
+            nc.scalar.activation(tanh_c[:], view(c_tiles, first, count), TANH)
+            nc.vector.tensor_mul(view(h_tiles, first, count), gate_o[:], tanh_c[:])
 
-        def leaves(first):
-            nodes = slice(first, first + PIECE)
-            pre_i = project(GATE_I, first, PIECE)
-            pre_u = project(GATE_U, first, PIECE)
-            pre_o = project(GATE_O, first, PIECE)
+        def leaves(first, pre_i, pre_u, pre_o):
             gate_i = work.tile([P, PIECE], F32, name="gate_i")
             gate_u = work.tile([P, PIECE], F32, name="gate_u")
             gate_o = work.tile([P, PIECE], F32, name="gate_o")
             nc.scalar.activation(gate_i[:], pre_i[:], SIGMOID, bias=b_sb[:, GATE_I : GATE_I + 1])
             nc.scalar.activation(gate_u[:], pre_u[:], TANH, bias=b_sb[:, GATE_U : GATE_U + 1])
-            nc.vector.tensor_mul(c[:, nodes], gate_i[:], gate_u[:])
+            nc.vector.tensor_mul(view(c_tiles, first, PIECE), gate_i[:], gate_u[:])
             nc.scalar.activation(gate_o[:], pre_o[:], SIGMOID, bias=b_sb[:, GATE_O : GATE_O + 1])
-            finish_cell(nodes, gate_o)
+            finish_cell(first, PIECE, gate_o)
 
         def project_upper(first, count):
             for gate in range(4):
@@ -120,9 +123,10 @@ def tile_treemodel_b_kernel(tc, table, w, b, u_iou, u_f, w_out, b_out, offs, out
 
         def level(first, count):
             nodes = slice(first, first + count)
-            kid0 = 2 * first + P
-            kids = slice(kid0, kid0 + 2 * count)
-            pairs = h[:, kids].rearrange("q (n two) -> q n two", two=2)
+            h_kids = view(h_tiles, 2 * first + P, 2 * count)
+            c_kids = view(c_tiles, 2 * first + P, 2 * count)
+            c_nodes = view(c_tiles, first, count)
+            pairs = h_kids.rearrange("q (n two) -> q n two", two=2)
             gates = {}
             for gate, func in ((GATE_I, SIGMOID), (GATE_U, TANH), (GATE_O, SIGMOID)):
                 bank = psum.tile([P, count], F32, name="bank", tag="bank")
@@ -137,62 +141,65 @@ def tile_treemodel_b_kernel(tc, table, w, b, u_iou, u_f, w_out, b_out, offs, out
                 gates[gate] = work.tile([P, count], F32, name="gate_%d" % gate)
                 nc.vector.tensor_add(gates[gate][:], bank[:], pre_sb[:, gate, nodes])
                 nc.scalar.activation(gates[gate][:], gates[gate][:], func)
-            forget = work.tile([P, 2 * count], F32, name="forget")
-            width = min(PIECE, 2 * count)
-            for k in range(0, 2 * count, width):
-                bank = psum.tile([P, width], F32, name="bank", tag="bank")
-                nc.tensor.matmul(bank[:], u_f_sb[:], h[:, kid0 + k : kid0 + k + width], start=True, stop=True)
-                parents = pre_sb[:, GATE_F, first + k // 2 : first + (k + width) // 2]
-                nc.vector.tensor_add(
-                    forget[:, k : k + width].rearrange("m (n two) -> m n two", two=2),
-                    bank[:].rearrange("m (n two) -> m n two", two=2),
-                    parents.unsqueeze(2).to_broadcast([P, width // 2, 2]),
-                )
+            bank = psum.tile([P, 2 * count], F32, name="bank", tag="bank")
+            nc.tensor.matmul(bank[:], u_f_sb[:], h_kids, start=True, stop=True)
+            forget = work.tile([P, count, 2], F32, name="forget")
+            nc.vector.tensor_add(
+                forget[:],
+                bank[:].rearrange("m (n two) -> m n two", two=2),
+                pre_sb[:, GATE_F, nodes].unsqueeze(2).to_broadcast([P, count, 2]),
+            )
             nc.scalar.activation(forget[:], forget[:], SIGMOID)
-            nc.vector.tensor_mul(forget[:], forget[:], c[:, kids])
-            kept = forget[:].rearrange("m (n two) -> m n two", two=2)
-            nc.vector.tensor_mul(c[:, nodes], gates[GATE_I][:], gates[GATE_U][:])
-            nc.vector.tensor_add(c[:, nodes], c[:, nodes], kept[:, :, 0])
-            nc.vector.tensor_add(c[:, nodes], c[:, nodes], kept[:, :, 1])
-            finish_cell(nodes, gates[GATE_O])
+            nc.vector.tensor_mul(forget[:], forget[:], c_kids.rearrange("m (n two) -> m n two", two=2))
+            nc.vector.tensor_mul(c_nodes, gates[GATE_I][:], gates[GATE_U][:])
+            nc.vector.tensor_add(c_nodes, c_nodes, forget[:, :, 0])
+            nc.vector.tensor_add(c_nodes, c_nodes, forget[:, :, 1])
+            finish_cell(first, count, gates[GATE_O])
 
-        def classify(block, first, count, staged, turn):
-            bank = psum.tile([P, count], F32, name="bank", tag="bank")
-            nc.tensor.matmul(
-                bank[:], w_out_sb[:, block * P : (block + 1) * P], h[:, first : first + count], start=True, stop=True
-            )
-            bias = b_out_sb[:, block : block + 1]
-            if turn == 0:
-                nc.scalar.activation(staged, bank[:], IDENTITY, bias=bias)
-            else:
-                nc.vector.tensor_scalar_add(staged, bank[:], bias)
-
-        def classify_leaves(block):
-            stage = stage_pool.tile([P, 2, PIECE], F32, name="stage")
-            for turn in range(2):
-                classify(block, LEAVES + turn * PIECE, PIECE, stage[:, turn, :], turn)
-            nc.sync.dma_start(out[block * P : (block + 1) * P, LEAVES:N], stage[:].rearrange("p t n -> p (t n)"))
-
-        def classify_upper(block, first, count):
-            stage = stage_pool.tile([P, 2, count], F32, name="stage")
-            for turn in range(2):
-                classify(block + turn, first, count, stage[:, turn, :], turn)
+        def classify(blocks, first, count, scalar_helps=True):
+            stage = stage_pool.tile([P, len(blocks), count], F32, name="stage")
+            turn = 0
+            for t, block in enumerate(blocks):
+                for k in range(0, count, PIECE):
+                    width = min(PIECE, count - k)
+                    bank = psum.tile([P, width], F32, name="bank", tag="bank")
+                    nc.tensor.matmul(
+                        bank[:],
+                        w_out_sb[:, block * P : (block + 1) * P],
+                        view(h_tiles, first + k, width),
+                        start=True,
+                        stop=True,
+                    )
+                    staged = stage[:, t, k : k + width]
+                    bias = b_out_sb[:, block : block + 1]
+                    if scalar_helps and turn % 2 == 0:
+                        nc.scalar.activation(staged, bank[:], IDENTITY, bias=bias)
+                    else:
+                        nc.vector.tensor_scalar_add(staged, bank[:], bias)
+                    turn += 1
             nc.sync.dma_start(
-                out[block * P : (block + 2) * P, first : first + count].rearrange("(t p) n -> p t n", p=P), stage[:]
+                out[blocks.start * P : blocks.stop * P, first : first + count].rearrange("(t p) n -> p t n", p=P),
+                stage[:],
             )
 
-        for first in range(LEAVES, N, PIECE):
-            leaves(first)
-        for block in range(EARLY_BLOCKS):
-            classify_leaves(block)
+        pieces = range(LEAVES, N, PIECE)
+        looked_up = [[project(gate, first, PIECE) for gate in (GATE_I, GATE_U, GATE_O)] for first in pieces]
+        for first, banks in zip(pieces, looked_up):
+            leaves(first, *banks)
+        for block in range(FIRST_BLOCKS):
+            classify(range(block, block + 1), LEAVES, PIECE, scalar_helps=False)
+        classify(range(FIRST_BLOCKS), LEAVES + PIECE, PIECE)
+        for block in range(FIRST_BLOCKS, EARLY_BLOCKS, 2):
+            classify(range(block, block + 2), LEAVES, N - LEAVES)
         project_upper(LEVEL2, LEAVES - LEVEL2)
         project_upper(0, LEVEL2)
-        level(LEVEL2, LEAVES - LEVEL2)
+        for first in range(LEVEL2, LEAVES, PIECE // 2):
+            level(first, PIECE // 2)
         level(LEVEL1, LEVEL2 - LEVEL1)
         level(0, LEVEL1)
-        for block in range(EARLY_BLOCKS, BLOCKS):
-            classify_leaves(block)
-        for block in range(0, BLOCKS, 2):
-            classify_upper(block, LEVEL2, LEAVES - LEVEL2)
-        for block in range(0, BLOCKS, 2):
-            classify_upper(block, 0, LEVEL2)
+        for block in range(EARLY_BLOCKS, BLOCKS, 2):
+            classify(range(block, block + 2), LEAVES, N - LEAVES)
+        for block in range(0, BLOCKS, 4):
+            classify(range(block, block + 4), LEVEL2, LEAVES - LEVEL2)
+        for block in range(0, BLOCKS, 4):
+            classify(range(block, block + 4), 0, LEVEL2)

@@ -29,7 +29,7 @@ def tile_treemodel_b_kernel(tc, table, w, b, u_iou, u_f, w_out, b_out, offs, out
         tc.tile_pool(name="rows", bufs=4) as rows_pool,
         tc.tile_pool(name="work", bufs=2) as work,
         tc.tile_pool(name="stage", bufs=17) as stage_pool,
-        tc.psum_pool(name="psum", bufs=8) as psum,
+        tc.psum_pool(name="psum", bufs=6) as psum,
     ):
         loaded = []
         for g in range(WORDS // (UNITS * FLIP)):
@@ -129,7 +129,7 @@ def tile_treemodel_b_kernel(tc, table, w, b, u_iou, u_f, w_out, b_out, offs, out
             pairs = h_kids.rearrange("q (n two) -> q n two", two=2)
             gates = {}
             for gate, func in ((GATE_I, SIGMOID), (GATE_U, TANH), (GATE_O, SIGMOID)):
-                bank = psum.tile([P, count], F32, name="bank", tag="bank")
+                bank = psum.tile([P, count], F32, name="climb", tag="climb", bufs=2)
                 for child in range(2):
                     nc.tensor.matmul(
                         bank[:],
@@ -141,7 +141,7 @@ def tile_treemodel_b_kernel(tc, table, w, b, u_iou, u_f, w_out, b_out, offs, out
                 gates[gate] = work.tile([P, count], F32, name="gate_%d" % gate)
                 nc.vector.tensor_add(gates[gate][:], bank[:], pre_sb[:, gate, nodes])
                 nc.scalar.activation(gates[gate][:], gates[gate][:], func)
-            bank = psum.tile([P, 2 * count], F32, name="bank", tag="bank")
+            bank = psum.tile([P, 2 * count], F32, name="climb", tag="climb", bufs=2)
             nc.tensor.matmul(bank[:], u_f_sb[:], h_kids, start=True, stop=True)
             forget = work.tile([P, count, 2], F32, name="forget")
             nc.vector.tensor_add(

@@ -8,15 +8,16 @@ IDENTITY = mybir.ActivationFunctionType.Identity
 
 P = 128
 WORDS, CLASSES, N = 4096, 4096, 1920
-GATE_I, GATE_O, GATE_U, GATE_F = 0, 1, 2, 3
 LEVEL1, LEVEL2, LEAVES = 128, 384, 896
+GATE_I, GATE_O, GATE_U, GATE_F = 0, 1, 2, 3
+CELL_GATES = ((GATE_I, SIGMOID), (GATE_U, TANH), (GATE_O, SIGMOID))
 PIECE = 512
 BLOCKS = CLASSES // P
 ROWS = 4
 FLIP = P * ROWS
 UNITS = 2
-SPANS = ((0, LEVEL2), (LEVEL2, PIECE), (LEAVES, PIECE), (LEAVES + PIECE, PIECE))
 FIRST_BLOCKS = 4
+BRIDGE_BLOCKS = 4
 EARLY_BLOCKS = 16
 
 FLOPS = 2 * P * (4 * P * N + 3 * P * LEAVES + P * 2 * LEAVES + CLASSES * N)
@@ -26,20 +27,20 @@ def tile_treemodel_b_kernel(tc, table, w, b, u_iou, u_f, w_out, b_out, offs, out
     nc = tc.nc
     with (
         tc.tile_pool(name="held", bufs=1) as held,
-        tc.tile_pool(name="rows", bufs=4) as rows_pool,
+        tc.tile_pool(name="chunks", bufs=WORDS // (UNITS * FLIP)) as chunks,
         tc.tile_pool(name="work", bufs=2) as work,
-        tc.tile_pool(name="stage", bufs=17) as stage_pool,
+        tc.tile_pool(name="stages", bufs=8) as stages,
         tc.psum_pool(name="psum", bufs=6) as psum,
     ):
-        loaded = []
-        for g in range(WORDS // (UNITS * FLIP)):
-            rows = rows_pool.tile([P, UNITS, ROWS * P], BF16, name="rows")
-            queue = nc.sync if g % 2 == 0 else nc.scalar
+        table_t = held.tile([P, WORDS], BF16, name="table_t")
+        units = []
+        for load, first in enumerate(range(0, WORDS, UNITS * FLIP)):
+            chunk = chunks.tile([P, UNITS, ROWS * P], BF16, name="chunk")
+            queue = nc.sync if load % 2 == 0 else nc.scalar
             queue.dma_start(
-                rows[:],
-                table[g * UNITS * FLIP : (g + 1) * UNITS * FLIP, :].rearrange("(u p r) d -> p u (r d)", u=UNITS, r=ROWS),
+                chunk[:], table[first : first + UNITS * FLIP, :].rearrange("(u p r) d -> p u (r d)", u=UNITS, r=ROWS)
             )
-            loaded.append(rows)
+            units.extend(chunk[:, u, :] for u in range(UNITS))
 
         identity = held.tile([P, P], BF16, name="identity")
         make_identity(nc, identity[:])
@@ -47,10 +48,10 @@ def tile_treemodel_b_kernel(tc, table, w, b, u_iou, u_f, w_out, b_out, offs, out
         offsets = held.tile([P, N // 16], U16, name="offsets")
         nc.sync.dma_start(offsets[:], offs)
         w_sb = held.tile([P, 4 * P], BF16, name="w_sb")
-        nc.scalar.dma_start(w_sb[:], w)
+        nc.sync.dma_start(w_sb[:], w)
         b_sb = held.tile([P, 4], F32, name="b_sb")
         with nc.allow_non_contiguous_dma(reason="512 biases, one to a partition and gate"):
-            nc.scalar.dma_start(b_sb[:], b.rearrange("(g p) o -> p (g o)", p=P))
+            nc.sync.dma_start(b_sb[:], b.rearrange("(g p) o -> p (g o)", p=P))
         w_out_sb = held.tile([P, CLASSES], BF16, name="w_out_sb")
         nc.sync.dma_start(w_out_sb[:], w_out)
         b_out_rows = held.tile([P, BLOCKS], F32, name="b_out_rows", align_bytes=64)
@@ -63,26 +64,20 @@ def tile_treemodel_b_kernel(tc, table, w, b, u_iou, u_f, w_out, b_out, offs, out
         u_f_sb = held.tile([P, P], BF16, name="u_f_sb")
         nc.gpsimd.dma_start(u_f_sb[:], u_f)
 
-        table_t = held.tile([P, WORDS], BF16, name="table_t")
-        for f in range(WORDS // FLIP):
-            rows = loaded[f // UNITS][:, f % UNITS, :]
+        for f, unit in enumerate(units):
             flipped = psum.tile([P, FLIP], BF16, name="flipped", tag="bank")
             for r in range(ROWS):
-                nc.tensor.transpose(flipped[:, r * P : (r + 1) * P], rows[:, r * P : (r + 1) * P], identity[:])
-            nc.vector.tensor_copy(
-                table_t[:, f * FLIP : (f + 1) * FLIP].rearrange("d (p r) -> d p r", r=ROWS),
-                flipped[:].rearrange("d (r p) -> d p r", r=ROWS),
-            )
-
+                nc.tensor.transpose(flipped[:, r * P : (r + 1) * P], unit[:, r * P : (r + 1) * P], identity[:])
+            words = table_t[:, f * FLIP : (f + 1) * FLIP].rearrange("d (p r) -> d p r", r=ROWS)
+            turned = flipped[:].rearrange("d (r p) -> d p r", r=ROWS)
+            if f % 3 == 1:
+                nc.scalar.copy(words, turned)
+            else:
+                nc.vector.tensor_copy(words, turned)
         nc.vector.transpose(b_out_sb[:], b_out_rows[:])
 
-        h_tiles = {first: held.tile([P, count], BF16, name="h_%d" % first) for first, count in SPANS}
-        c_tiles = {first: held.tile([P, count], F32, name="c_%d" % first) for first, count in SPANS}
-
-        def view(tiles, first, count):
-            for start, width in SPANS:
-                if start <= first and first + count <= start + width:
-                    return tiles[start][:, first - start : first - start + count]
+        h = held.tile([P, N], BF16, name="h")
+        c = held.tile([P, N], F32, name="c")
         pre_sb = held.tile([P, 4, LEAVES], F32, name="pre_sb")
 
         def project(gate, first, count):
@@ -96,20 +91,19 @@ def tile_treemodel_b_kernel(tc, table, w, b, u_iou, u_f, w_out, b_out, offs, out
             )
             return bank
 
-        def finish_cell(first, count, gate_o):
-            tanh_c = work.tile([P, count], F32, name="tanh_c")
-            nc.scalar.activation(tanh_c[:], view(c_tiles, first, count), TANH)
-            nc.vector.tensor_mul(view(h_tiles, first, count), gate_o[:], tanh_c[:])
+        def finish_cell(nodes, gate_o):
+            tanh_c = work.tile([P, nodes.stop - nodes.start], F32, name="tanh_c")
+            nc.scalar.activation(tanh_c[:], c[:, nodes], TANH)
+            nc.vector.tensor_mul(h[:, nodes], gate_o[:], tanh_c[:])
 
-        def leaves(first, pre_i, pre_u, pre_o):
-            gate_i = work.tile([P, PIECE], F32, name="gate_i")
-            gate_u = work.tile([P, PIECE], F32, name="gate_u")
-            gate_o = work.tile([P, PIECE], F32, name="gate_o")
-            nc.scalar.activation(gate_i[:], pre_i[:], SIGMOID, bias=b_sb[:, GATE_I : GATE_I + 1])
-            nc.scalar.activation(gate_u[:], pre_u[:], TANH, bias=b_sb[:, GATE_U : GATE_U + 1])
-            nc.vector.tensor_mul(view(c_tiles, first, PIECE), gate_i[:], gate_u[:])
-            nc.scalar.activation(gate_o[:], pre_o[:], SIGMOID, bias=b_sb[:, GATE_O : GATE_O + 1])
-            finish_cell(first, PIECE, gate_o)
+        def leaves(first, count, banks):
+            nodes = slice(first, first + count)
+            gates = {}
+            for gate, func in CELL_GATES:
+                gates[gate] = work.tile([P, count], F32, name="gate_%d" % gate)
+                nc.scalar.activation(gates[gate][:], banks[gate][:], func, bias=b_sb[:, gate : gate + 1])
+            nc.vector.tensor_mul(c[:, nodes], gates[GATE_I][:], gates[GATE_U][:])
+            finish_cell(nodes, gates[GATE_O])
 
         def project_upper(first, count):
             for gate in range(4):
@@ -123,26 +117,11 @@ def tile_treemodel_b_kernel(tc, table, w, b, u_iou, u_f, w_out, b_out, offs, out
 
         def level(first, count):
             nodes = slice(first, first + count)
-            h_kids = view(h_tiles, 2 * first + P, 2 * count)
-            c_kids = view(c_tiles, 2 * first + P, 2 * count)
-            c_nodes = view(c_tiles, first, count)
-            pairs = h_kids.rearrange("q (n two) -> q n two", two=2)
-            gates = {}
-            for gate, func in ((GATE_I, SIGMOID), (GATE_U, TANH), (GATE_O, SIGMOID)):
-                bank = psum.tile([P, count], F32, name="climb", tag="climb", bufs=2)
-                for child in range(2):
-                    nc.tensor.matmul(
-                        bank[:],
-                        u_iou_sb[:, gate * P : (gate + 1) * P],
-                        pairs[:, :, child],
-                        start=(child == 0),
-                        stop=(child == 1),
-                    )
-                gates[gate] = work.tile([P, count], F32, name="gate_%d" % gate)
-                nc.vector.tensor_add(gates[gate][:], bank[:], pre_sb[:, gate, nodes])
-                nc.scalar.activation(gates[gate][:], gates[gate][:], func)
+            kids = slice(2 * first + P, 2 * first + P + 2 * count)
+            h_pairs = h[:, kids].rearrange("q (n two) -> q n two", two=2)
+            c_pairs = c[:, kids].rearrange("m (n two) -> m n two", two=2)
             bank = psum.tile([P, 2 * count], F32, name="climb", tag="climb", bufs=2)
-            nc.tensor.matmul(bank[:], u_f_sb[:], h_kids, start=True, stop=True)
+            nc.tensor.matmul(bank[:], u_f_sb[:], h[:, kids], start=True, stop=True)
             forget = work.tile([P, count, 2], F32, name="forget")
             nc.vector.tensor_add(
                 forget[:],
@@ -150,15 +129,29 @@ def tile_treemodel_b_kernel(tc, table, w, b, u_iou, u_f, w_out, b_out, offs, out
                 pre_sb[:, GATE_F, nodes].unsqueeze(2).to_broadcast([P, count, 2]),
             )
             nc.scalar.activation(forget[:], forget[:], SIGMOID)
-            nc.vector.tensor_mul(forget[:], forget[:], c_kids.rearrange("m (n two) -> m n two", two=2))
-            nc.vector.tensor_mul(c_nodes, gates[GATE_I][:], gates[GATE_U][:])
-            nc.vector.tensor_add(c_nodes, c_nodes, forget[:, :, 0])
-            nc.vector.tensor_add(c_nodes, c_nodes, forget[:, :, 1])
-            finish_cell(first, count, gates[GATE_O])
+            nc.vector.tensor_mul(forget[:], forget[:], c_pairs)
+            gates = {}
+            for gate, func in CELL_GATES:
+                bank = psum.tile([P, count], F32, name="climb", tag="climb", bufs=2)
+                for child in range(2):
+                    nc.tensor.matmul(
+                        bank[:],
+                        u_iou_sb[:, gate * P : (gate + 1) * P],
+                        h_pairs[:, :, child],
+                        start=(child == 0),
+                        stop=(child == 1),
+                    )
+                gates[gate] = work.tile([P, count], F32, name="gate_%d" % gate)
+                nc.vector.tensor_add(gates[gate][:], bank[:], pre_sb[:, gate, nodes])
+                nc.scalar.activation(gates[gate][:], gates[gate][:], func)
+                if gate == GATE_U:
+                    nc.vector.tensor_mul(c[:, nodes], gates[GATE_I][:], gates[GATE_U][:])
+                    for child in range(2):
+                        nc.vector.tensor_add(c[:, nodes], c[:, nodes], forget[:, :, child])
+            finish_cell(nodes, gates[GATE_O])
 
         def classify(blocks, first, count, scalar_helps=True):
-            stage = stage_pool.tile([P, len(blocks), count], F32, name="stage")
-            turn = 0
+            stage = stages.tile([P, len(blocks), count], F32, name="stage", align_bytes=256)
             for t, block in enumerate(blocks):
                 for k in range(0, count, PIECE):
                     width = min(PIECE, count - k)
@@ -166,40 +159,38 @@ def tile_treemodel_b_kernel(tc, table, w, b, u_iou, u_f, w_out, b_out, offs, out
                     nc.tensor.matmul(
                         bank[:],
                         w_out_sb[:, block * P : (block + 1) * P],
-                        view(h_tiles, first + k, width),
+                        h[:, first + k : first + k + width],
                         start=True,
                         stop=True,
                     )
                     staged = stage[:, t, k : k + width]
                     bias = b_out_sb[:, block : block + 1]
-                    if scalar_helps and turn % 2 == 0:
-                        nc.scalar.activation(staged, bank[:], IDENTITY, bias=bias)
+                    if scalar_helps:
+                        nc.any.tensor_scalar_add(staged, bank[:], bias)
                     else:
                         nc.vector.tensor_scalar_add(staged, bank[:], bias)
-                    turn += 1
             nc.sync.dma_start(
                 out[blocks.start * P : blocks.stop * P, first : first + count].rearrange("(t p) n -> p t n", p=P),
                 stage[:],
             )
 
-        pieces = range(LEAVES, N, PIECE)
-        looked_up = [[project(gate, first, PIECE) for gate in (GATE_I, GATE_U, GATE_O)] for first in pieces]
-        for first, banks in zip(pieces, looked_up):
-            leaves(first, *banks)
-        for block in range(FIRST_BLOCKS):
-            classify(range(block, block + 1), LEAVES, PIECE, scalar_helps=False)
-        classify(range(FIRST_BLOCKS), LEAVES + PIECE, PIECE)
+        pieces = ((LEAVES, PIECE // 2), (LEAVES + PIECE // 2, PIECE // 2), (LEAVES + PIECE, PIECE))
+        looked_up = [{gate: project(gate, first, count) for gate, func in CELL_GATES} for first, count in pieces]
+        for (first, count), banks in zip(pieces, looked_up):
+            leaves(first, count, banks)
+        for first, count in pieces:
+            for block in range(0, FIRST_BLOCKS, 2):
+                classify(range(block, block + 2), first, count, scalar_helps=(count == PIECE))
         for block in range(FIRST_BLOCKS, EARLY_BLOCKS, 2):
             classify(range(block, block + 2), LEAVES, N - LEAVES)
         project_upper(LEVEL2, LEAVES - LEVEL2)
         project_upper(0, LEVEL2)
-        for first in range(LEVEL2, LEAVES, PIECE // 2):
-            level(first, PIECE // 2)
-        level(LEVEL1, LEVEL2 - LEVEL1)
-        level(0, LEVEL1)
-        for block in range(EARLY_BLOCKS, BLOCKS, 2):
-            classify(range(block, block + 2), LEAVES, N - LEAVES)
-        for block in range(0, BLOCKS, 4):
-            classify(range(block, block + 4), LEVEL2, LEAVES - LEVEL2)
-        for block in range(0, BLOCKS, 4):
-            classify(range(block, block + 4), 0, LEVEL2)
+        for first, count in ((LEVEL2, LEAVES - LEVEL2), (LEVEL1, LEVEL2 - LEVEL1), (0, LEVEL1)):
+            for half in range(2):
+                level(first + half * (count // 2), count // 2)
+        for block in range(EARLY_BLOCKS, BLOCKS, 4):
+            classify(range(block, block + 4), LEAVES, N - LEAVES)
+        classify(range(BRIDGE_BLOCKS), LEVEL2, LEAVES - LEVEL2)
+        for block in range(BRIDGE_BLOCKS, BLOCKS, 4):
+            classify(range(block, block + 4), 0, LEAVES)
+        classify(range(BRIDGE_BLOCKS), 0, LEVEL2)

import concourse.mybir as mybir
from concourse.masks import make_identity

BF16, F32, U16 = mybir.dt.bfloat16, mybir.dt.float32, mybir.dt.uint16
SIGMOID = mybir.ActivationFunctionType.Sigmoid
TANH = mybir.ActivationFunctionType.Tanh
IDENTITY = mybir.ActivationFunctionType.Identity

P = 128
WORDS, CLASSES, N = 4096, 4096, 1920
LEVEL1, LEVEL2, LEAVES = 128, 384, 896
GATE_I, GATE_O, GATE_U, GATE_F = 0, 1, 2, 3
CELL_GATES = ((GATE_I, SIGMOID), (GATE_U, TANH), (GATE_O, SIGMOID))
PIECE = 512
BLOCKS = CLASSES // P
ROWS = 4
FLIP = P * ROWS
UNITS = 2
FIRST_BLOCKS = 4
BRIDGE_BLOCKS = 4
EARLY_BLOCKS = 16

FLOPS = 2 * P * (4 * P * N + 3 * P * LEAVES + P * 2 * LEAVES + CLASSES * N)


def tile_treemodel_b_kernel(tc, table, w, b, u_iou, u_f, w_out, b_out, offs, out):
    nc = tc.nc
    with (
        tc.tile_pool(name="held", bufs=1) as held,
        tc.tile_pool(name="chunks", bufs=WORDS // (UNITS * FLIP)) as chunks,
        tc.tile_pool(name="work", bufs=2) as work,
        tc.tile_pool(name="stages", bufs=8) as stages,
        tc.psum_pool(name="psum", bufs=6) as psum,
    ):
        table_t = held.tile([P, WORDS], BF16, name="table_t")
        units = []
        for load, first in enumerate(range(0, WORDS, UNITS * FLIP)):
            chunk = chunks.tile([P, UNITS, ROWS * P], BF16, name="chunk")
            queue = nc.sync if load % 2 == 0 else nc.scalar
            queue.dma_start(
                chunk[:], table[first : first + UNITS * FLIP, :].rearrange("(u p r) d -> p u (r d)", u=UNITS, r=ROWS)
            )
            units.extend(chunk[:, u, :] for u in range(UNITS))

        identity = held.tile([P, P], BF16, name="identity")
        make_identity(nc, identity[:])

        offsets = held.tile([P, N // 16], U16, name="offsets")
        nc.sync.dma_start(offsets[:], offs)
        w_sb = held.tile([P, 4 * P], BF16, name="w_sb")
        nc.sync.dma_start(w_sb[:], w)
        b_sb = held.tile([P, 4], F32, name="b_sb")
        with nc.allow_non_contiguous_dma(reason="512 biases, one to a partition and gate"):
            nc.sync.dma_start(b_sb[:], b.rearrange("(g p) o -> p (g o)", p=P))
        w_out_sb = held.tile([P, CLASSES], BF16, name="w_out_sb")
        nc.sync.dma_start(w_out_sb[:], w_out)
        b_out_rows = held.tile([P, BLOCKS], F32, name="b_out_rows", align_bytes=64)
        b_out_sb = held.tile([P, BLOCKS], F32, name="b_out_sb", align_bytes=64)
        b_out_view = b_out.rearrange("(a q i) o -> q a (i o)", q=4, i=32)
        for q in range(4):
            nc.gpsimd.dma_start(b_out_rows[32 * q : 32 * (q + 1), :], b_out_view[q])
        u_iou_sb = held.tile([P, 3 * P], BF16, name="u_iou_sb")
        nc.gpsimd.dma_start(u_iou_sb[:], u_iou)
        u_f_sb = held.tile([P, P], BF16, name="u_f_sb")
        nc.gpsimd.dma_start(u_f_sb[:], u_f)

        for f, unit in enumerate(units):
            flipped = psum.tile([P, FLIP], BF16, name="flipped", tag="bank")
            for r in range(ROWS):
                nc.tensor.transpose(flipped[:, r * P : (r + 1) * P], unit[:, r * P : (r + 1) * P], identity[:])
            words = table_t[:, f * FLIP : (f + 1) * FLIP].rearrange("d (p r) -> d p r", r=ROWS)
            turned = flipped[:].rearrange("d (r p) -> d p r", r=ROWS)
            if f % 3 == 1:
                nc.scalar.copy(words, turned)
            else:
                nc.vector.tensor_copy(words, turned)
        nc.vector.transpose(b_out_sb[:], b_out_rows[:])

        h = held.tile([P, N], BF16, name="h")
        c = held.tile([P, N], F32, name="c")
        pre_sb = held.tile([P, 4, LEAVES], F32, name="pre_sb")

        def project(gate, first, count):
            bank = psum.tile([P, count], F32, name="bank", tag="bank")
            nc.tensor.matmul(
                bank[:],
                w_sb[:, gate * P : (gate + 1) * P],
                table_t[:].indirect(offsets[:, first // 16 : (first + count) // 16]),
                start=True,
                stop=True,
            )
            return bank

        def finish_cell(nodes, gate_o):
            tanh_c = work.tile([P, nodes.stop - nodes.start], F32, name="tanh_c")
            nc.scalar.activation(tanh_c[:], c[:, nodes], TANH)
            nc.vector.tensor_mul(h[:, nodes], gate_o[:], tanh_c[:])

        def leaves(first, count, banks):
            nodes = slice(first, first + count)
            gates = {}
            for gate, func in CELL_GATES:
                gates[gate] = work.tile([P, count], F32, name="gate_%d" % gate)
                nc.scalar.activation(gates[gate][:], banks[gate][:], func, bias=b_sb[:, gate : gate + 1])
            nc.vector.tensor_mul(c[:, nodes], gates[GATE_I][:], gates[GATE_U][:])
            finish_cell(nodes, gates[GATE_O])

        def project_upper(first, count):
            for gate in range(4):
                bank = project(gate, first, count)
                kept = pre_sb[:, gate, first : first + count]
                bias = b_sb[:, gate : gate + 1]
                if gate % 2 == 0:
                    nc.scalar.activation(kept, bank[:], IDENTITY, bias=bias)
                else:
                    nc.vector.tensor_scalar_add(kept, bank[:], bias)

        def level(first, count):
            nodes = slice(first, first + count)
            kids = slice(2 * first + P, 2 * first + P + 2 * count)
            h_pairs = h[:, kids].rearrange("q (n two) -> q n two", two=2)
            c_pairs = c[:, kids].rearrange("m (n two) -> m n two", two=2)
            bank = psum.tile([P, 2 * count], F32, name="climb", tag="climb", bufs=2)
            nc.tensor.matmul(bank[:], u_f_sb[:], h[:, kids], start=True, stop=True)
            forget = work.tile([P, count, 2], F32, name="forget")
            nc.vector.tensor_add(
                forget[:],
                bank[:].rearrange("m (n two) -> m n two", two=2),
                pre_sb[:, GATE_F, nodes].unsqueeze(2).to_broadcast([P, count, 2]),
            )
            nc.scalar.activation(forget[:], forget[:], SIGMOID)
            nc.vector.tensor_mul(forget[:], forget[:], c_pairs)
            gates = {}
            for gate, func in CELL_GATES:
                bank = psum.tile([P, count], F32, name="climb", tag="climb", bufs=2)
                for child in range(2):
                    nc.tensor.matmul(
                        bank[:],
                        u_iou_sb[:, gate * P : (gate + 1) * P],
                        h_pairs[:, :, child],
                        start=(child == 0),
                        stop=(child == 1),
                    )
                gates[gate] = work.tile([P, count], F32, name="gate_%d" % gate)
                nc.vector.tensor_add(gates[gate][:], bank[:], pre_sb[:, gate, nodes])
                nc.scalar.activation(gates[gate][:], gates[gate][:], func)
                if gate == GATE_U:
                    nc.vector.tensor_mul(c[:, nodes], gates[GATE_I][:], gates[GATE_U][:])
                    for child in range(2):
                        nc.vector.tensor_add(c[:, nodes], c[:, nodes], forget[:, :, child])
            finish_cell(nodes, gates[GATE_O])

        def classify(blocks, first, count, scalar_helps=True):
            stage = stages.tile([P, len(blocks), count], F32, name="stage", align_bytes=256)
            for t, block in enumerate(blocks):
                for k in range(0, count, PIECE):
                    width = min(PIECE, count - k)
                    bank = psum.tile([P, width], F32, name="bank", tag="bank")
                    nc.tensor.matmul(
                        bank[:],
                        w_out_sb[:, block * P : (block + 1) * P],
                        h[:, first + k : first + k + width],
                        start=True,
                        stop=True,
                    )
                    staged = stage[:, t, k : k + width]
                    bias = b_out_sb[:, block : block + 1]
                    if scalar_helps:
                        nc.any.tensor_scalar_add(staged, bank[:], bias)
                    else:
                        nc.vector.tensor_scalar_add(staged, bank[:], bias)
            nc.sync.dma_start(
                out[blocks.start * P : blocks.stop * P, first : first + count].rearrange("(t p) n -> p t n", p=P),
                stage[:],
            )

        pieces = ((LEAVES, PIECE // 2), (LEAVES + PIECE // 2, PIECE // 2), (LEAVES + PIECE, PIECE))
        looked_up = [{gate: project(gate, first, count) for gate, func in CELL_GATES} for first, count in pieces]
        for (first, count), banks in zip(pieces, looked_up):
            leaves(first, count, banks)
        for first, count in pieces:
            for block in range(0, FIRST_BLOCKS, 2):
                classify(range(block, block + 2), first, count, scalar_helps=(count == PIECE))
        for block in range(FIRST_BLOCKS, EARLY_BLOCKS, 2):
            classify(range(block, block + 2), LEAVES, N - LEAVES)
        project_upper(LEVEL2, LEAVES - LEVEL2)
        project_upper(0, LEVEL2)
        for first, count in ((LEVEL2, LEAVES - LEVEL2), (LEVEL1, LEVEL2 - LEVEL1), (0, LEVEL1)):
            for half in range(2):
                level(first + half * (count // 2), count // 2)
        for block in range(EARLY_BLOCKS, BLOCKS, 4):
            classify(range(block, block + 4), LEAVES, N - LEAVES)
        classify(range(BRIDGE_BLOCKS), LEVEL2, LEAVES - LEVEL2)
        for block in range(BRIDGE_BLOCKS, BLOCKS, 4):
            classify(range(block, block + 4), 0, LEAVES)
        classify(range(BRIDGE_BLOCKS), 0, LEVEL2)
